import numpy as np
import ml_dtypes


def mxq(x, axis, fmt="e4m3"):
    dtype, down = {"e4m3": (ml_dtypes.float8_e4m3fn, 7), "e5m2": (ml_dtypes.float8_e5m2, 14)}[fmt]
    v = np.moveaxis(np.asarray(x, np.float32).astype(ml_dtypes.bfloat16).astype(np.float64), axis, -1)
    blocks = v.reshape(v.shape[:-1] + (-1, 32))
    amax = np.abs(blocks).max(-1, keepdims=True)
    byte = np.maximum(np.where(amax > 0, np.frexp(amax)[1] - 1 + 127, 0) - down, 1)
    scale = np.exp2(byte - 127.0)
    codes = (blocks / scale).astype(np.float32).astype(dtype).astype(np.float64)
    return np.moveaxis((codes * scale).reshape(v.shape), -1, axis)


WIDE = False


def mx_kscale(k):
    if not WIDE:
        return np.ones(k)
    levels = np.array([10, -10, 5, -5, 0])
    a = np.random.permutation(np.resize(levels, k // 512 * 4)).reshape(k // 512, 4)
    idx = np.arange(k)
    return np.exp2(a[idx // 512, idx % 128 // 32])


BF16 = ml_dtypes.bfloat16


def bf(x):
    return np.asarray(x, np.float32).astype(BF16)


def f64(x):
    return np.asarray(x).astype(np.float64)


E2M1 = np.array([0.0, 0.5, 1.0, 1.5, 2.0, 3.0, 4.0, 6.0, -0.0, -0.5, -1.0, -1.5, -2.0, -3.0, -4.0, -6.0])


def pack_weight(w, fmt):
    k, n = w.shape
    w = f64(bf(w)).reshape(k // 32, 32, n)
    amax = np.abs(w).max(1)
    if fmt == "e4m3":
        byte = np.frexp(amax)[1] - 1 + 127 - 7
    else:
        mant, ex = np.frexp(amax / 6.0)
        byte = np.where(mant > 0.5, ex, ex - 1) + 127
    byte = np.clip(np.where(amax > 0, byte, 1), 1, 254)
    scaled = (w * np.exp2(127.0 - byte)[:, None, :]).reshape(k, n).astype(np.float32)
    by_word = np.ascontiguousarray(scaled.reshape(k // 512, 128, 4, n).transpose(0, 1, 3, 2))
    if fmt == "e4m3":
        words = by_word.astype(ml_dtypes.float8_e4m3fn).view(np.uint8)
    else:
        c = by_word.astype(ml_dtypes.float4_e2m1fn).view(np.uint8) & 0xF
        words = c[..., 0::2] | (c[..., 1::2] << 4)
    return np.ascontiguousarray(words), np.ascontiguousarray(byte.astype(np.uint8).reshape(k // 512, 16, n))


def unpack_weight(words, scales, fmt):
    g, p, n, _ = words.shape
    if fmt == "e4m3":
        vals = np.ascontiguousarray(words).view(ml_dtypes.float8_e4m3fn).astype(np.float64)
    else:
        nib = np.empty((g, p, n, 4), np.uint8)
        nib[..., 0::2] = words & 0xF
        nib[..., 1::2] = words >> 4
        vals = E2M1[nib]
    vals = vals * np.repeat(np.exp2(scales.astype(np.float64) - 127.0), 8, axis=1)[..., None]
    return vals.transpose(0, 1, 3, 2).reshape(g * 512, n)

def pack4(w):
    words, scales = pack_weight(w, "e2m1")
    return words.reshape(words.shape[0], 128, -1), scales


def unpack4(words, scales):
    return unpack_weight(words.reshape(words.shape[0], 128, -1, 2), scales, "e2m1")


B, T, HP, WP, NH, D, DFF = 16, 8, 6, 6, 16, 512, 4096
HW = HP * WP


def setup_inputs():
    s = mx_kscale(D)
    c = np.random.standard_normal((B * T, 1 + HW, D)) * 1.5 / np.sqrt(1 + HW)
    c[:, 0, :] *= 5.0
    ctx_s = bf(c * s)
    x_res = bf(np.random.standard_normal((B, 1 + HW * T, D)) * 1.1)
    words, scales = pack4(np.random.standard_normal((D, D)) / np.sqrt(D) / s[:, None])
    return {"ctx_s": ctx_s,
            "x_res": x_res,
            "s_out_w_words": words,
            "s_out_w_scales": scales,
            "s_out_b": bf(0.1 * np.random.standard_normal(D))}


def reference(ctx_s, x_res, s_out_w_words, s_out_w_scales, s_out_b):
    res_s = (mxq(f64(ctx_s), 2, "e4m3") @ unpack4(s_out_w_words, s_out_w_scales)) + f64(s_out_b)
    cls_tok = res_s[:, 0, :].reshape(B, T, D).mean(axis=1, keepdims=True)
    res_p = res_s[:, 1:, :].reshape(B, T, HW, D).swapaxes(1, 2).reshape(B, HW * T, D)
    return f64(x_res) + np.concatenate([cls_tok, res_p], axis=1)

@@ -1,0 +1,193 @@
+from contextlib import ExitStack
+
+import concourse.mybir as mybir
+from concourse.masks import make_identity
+
+F32 = mybir.dt.float32
+BF16 = mybir.dt.bfloat16
+I32 = mybir.dt.int32
+U32 = mybir.dt.uint32
+U8 = mybir.dt.uint8
+FP8X4 = mybir.dt.float8_e4m3fn_x4
+FP4X4 = mybir.dt.float4_e2m1fn_x4
+ADD = mybir.AluOpType.add
+MULT = mybir.AluOpType.mult
+
+P = 128
+SAMPLES = 16
+FRAMES = 8
+PATCHES = 36
+POSITIONS = 1 + PATCHES
+WIDTH = 512
+PACK = 4
+WORDS = WIDTH // 2
+BATCH = 4
+BATCHES = [(0, 1)] + [(first, BATCH) for first in range(1, POSITIONS, BATCH)]
+VECTOR_EVERY = 3
+
+FLOPS = 2 * P * POSITIONS * WIDTH * WIDTH
+
+
+def tile_timesformerlayer_pc_t_kernel(
+    tc, ctx_s, x_res, s_out_w_words, s_out_w_scales, s_out_b, out
+):
+    nc = tc.nc
+    with ExitStack() as stack:
+        resident = stack.enter_context(tc.tile_pool(name="resident", bufs=1))
+        staging = stack.enter_context(tc.tile_pool(name="staging", bufs=3))
+        bias_bank = stack.enter_context(tc.psum_pool(name="bias_bank", bufs=1))
+        flipped_banks = stack.enter_context(tc.psum_pool(name="flipped_banks", bufs=3))
+        product_banks = stack.enter_context(tc.psum_pool(name="product_banks", bufs=4))
+
+        ctx_tiles = [
+            resident.tile([P, count, WIDTH], BF16, name="ctx%d" % first)
+            for first, count in BATCHES
+        ]
+        xres_tiles = [resident.tile([P, WIDTH], BF16, name="xres%d" % p) for p in range(PATCHES)]
+        sum_tiles = [resident.tile([P, WIDTH], F32, name="sum%d" % p) for p in range(PATCHES)]
+
+        nc.sync.dma_start(out=ctx_tiles[0][:], in_=ctx_s[:, 0:1, :])
+
+        w_words = resident.tile([P, 2 * WIDTH], U8, align_bytes=64)
+        nc.sync.dma_start(out=w_words[:].bitcast(I32), in_=s_out_w_words[0].bitcast(I32))
+        w_scales = resident.tile([P, WIDTH], U8, align_bytes=64)
+        nc.vector.memset(w_scales[:].bitcast(I32), 0)
+        for quadrant in range(4):
+            nc.sync.dma_start(
+                out=w_scales[32 * quadrant : 32 * quadrant + 4, :].bitcast(I32),
+                in_=s_out_w_scales[0, 4 * quadrant : 4 * quadrant + 4, :].bitcast(I32),
+            )
+
+        bias_row = resident.tile([P, WIDTH], BF16)
+        nc.vector.memset(bias_row[:], 0.0)
+        nc.sync.dma_start(out=bias_row[0:1, :], in_=s_out_b.unsqueeze(0))
+        xres_class = resident.tile([SAMPLES, WIDTH], BF16)
+        nc.sync.dma_start(out=xres_class[:], in_=x_res[:, 0, :])
+
+        for i in range(1, len(BATCHES)):
+            first, count = BATCHES[i]
+            nc.sync.dma_start(out=ctx_tiles[i][:], in_=ctx_s[:, first : first + count, :])
+            for p in range(first - 1, first - 1 + count):
+                nc.sync.dma_start(
+                    out=xres_tiles[p][:], in_=x_res[:, 1 + FRAMES * p : 1 + FRAMES * (p + 1), :]
+                )
+
+        identity = resident.tile([P, P], F32)
+        make_identity(nc, identity[:])
+
+        ones = resident.tile([P, P], BF16)
+        nc.vector.memset(ones[:], 1.0)
+        bias_psum = bias_bank.tile([P, WIDTH], F32)
+        nc.tensor.matmul(out=bias_psum[:], lhsT=ones[:], rhs=bias_row[:], start=True, stop=True)
+        bias_sbuf = resident.tile([P, WIDTH], F32)
+        nc.vector.tensor_copy(out=bias_sbuf[:], in_=bias_psum[:])
+
+        same_sample = resident.tile([P, P], F32)
+        nc.vector.memset(same_sample[:], 0.0)
+        nc.vector.tensor_reduce(
+            out=same_sample[:, 0:SAMPLES],
+            in_=identity[:].rearrange("k (b t) -> k b t", t=FRAMES),
+            axis=mybir.AxisListType.X,
+            op=ADD,
+        )
+
+        def transpose_batch(i):
+            count = BATCHES[i][1]
+            words = ctx_tiles[i][:].bitcast(F32)
+            grouped = staging.tile([P, count * P * PACK], BF16, tag="grouped", align_bytes=64)
+            grouped_words = grouped[:].bitcast(F32).rearrange("q (s u) -> q s u", u=2)
+            for j0 in range(0, count, 2):
+                n = min(2, count - j0)
+                flipped = flipped_banks.tile([P, 2, 2, P], F32, tag="flipped")
+                for j in range(n):
+                    for u in range(2):
+                        nc.tensor.transpose(
+                            flipped[:, j, u, :], words[:, j0 + j, u:WORDS:2], identity[:]
+                        )
+                nc.scalar.copy(
+                    out=grouped_words[:, j0 * P : (j0 + n) * P, :].rearrange(
+                        "q (j s) u -> q j s u", j=n
+                    ),
+                    in_=flipped[:, 0:n].rearrange("q j u s -> q j s u"),
+                )
+            return grouped
+
+        def quantise_batch(i, grouped):
+            count = BATCHES[i][1]
+            codes = staging.tile([P, count * P], U32, tag="codes", align_bytes=64)
+            scales = staging.tile([P, count * P], U8, tag="scales", align_bytes=64)
+            nc.vector.quantize_mx(out=codes[:].bitcast(FP8X4), scales=scales[:], in_=grouped[:])
+            return codes, scales
+
+        def multiply(quantised, j):
+            codes, scales = quantised
+            tokens = slice(j * P, (j + 1) * P)
+            product = product_banks.tile([P, WIDTH], F32, tag="product")
+            nc.tensor.matmul_mx(
+                out=product[:],
+                lhsT=codes[:, tokens].bitcast(FP8X4),
+                lhsT_scale=scales[:, tokens],
+                rhs=w_words[:].bitcast(FP4X4),
+                rhs_scale=w_scales[:],
+                start=True,
+                stop=True,
+            )
+            return product
+
+        def add_bias(p):
+            if p % VECTOR_EVERY == 0:
+                nc.vector.tensor_tensor(
+                    out=sum_tiles[p][:], in0=bias_psum[:], in1=xres_tiles[p][:], op=ADD
+                )
+            else:
+                nc.gpsimd.tensor_tensor(
+                    out=sum_tiles[p][:], in0=xres_tiles[p][:], in1=bias_sbuf[:], op=ADD
+                )
+
+        def finish_patch(p, product):
+            nc.vector.tensor_tensor(
+                out=sum_tiles[p][:], in0=product[:], in1=sum_tiles[p][:], op=ADD
+            )
+            nc.sync.dma_start(
+                out=out[:, 1 + FRAMES * p : 1 + FRAMES * (p + 1), :], in_=sum_tiles[p][:]
+            )
+
+        def finish_class_token(product):
+            class_res = resident.tile([P, WIDTH], F32)
+            nc.scalar.copy(out=class_res[:], in_=product[:])
+            frame_sum = product_banks.tile([P, WIDTH], F32, tag="product")
+            nc.tensor.matmul(
+                out=frame_sum[:], lhsT=same_sample[:], rhs=class_res[:], start=True, stop=True
+            )
+            class_sum = resident.tile([SAMPLES, WIDTH], F32)
+            nc.vector.tensor_tensor(
+                out=class_sum[:], in0=bias_psum[0:SAMPLES, :], in1=xres_class[:], op=ADD
+            )
+            nc.vector.scalar_tensor_tensor(
+                out=class_sum[:],
+                in0=frame_sum[0:SAMPLES, :],
+                scalar=1.0 / FRAMES,
+                in1=class_sum[:],
+                op0=MULT,
+                op1=ADD,
+            )
+            nc.sync.dma_start(out=out[:, 0, :], in_=class_sum[:])
+
+        last = len(BATCHES) - 1
+        grouped_tiles = {0: transpose_batch(0), 1: transpose_batch(1)}
+        products = [multiply(quantise_batch(0, grouped_tiles[0]), 0)]
+        for i in range(len(BATCHES)):
+            first, count = BATCHES[i]
+            if i + 2 <= last:
+                grouped_tiles[i + 2] = transpose_batch(i + 2)
+            if i + 1 <= last:
+                quantised = quantise_batch(i + 1, grouped_tiles[i + 1])
+                for j in range(BATCH):
+                    add_bias(BATCHES[i + 1][0] - 1 + j)
+            if i == 0:
+                finish_class_token(products[0])
+            else:
+                for j in range(count):
+                    finish_patch(first - 1 + j, products[j])
+            if i + 1 <= last:
+                products = [multiply(quantised, j) for j in range(BATCH)]

@@ -94,6 +94,8 @@ def tile_timesformerlayer_pc_t_kernel(
         def transpose_batch(i):
             count = BATCHES[i][1]
             words = ctx_tiles[i][:].bitcast(F32)
+            split = staging.tile([P, count, 2, P], F32, tag="split")
+            nc.scalar.copy(out=split[:], in_=words.rearrange("s j (q u) -> s j u q", u=2))
             grouped = staging.tile([P, count * P * PACK], BF16, tag="grouped", align_bytes=64)
             grouped_words = grouped[:].bitcast(F32).rearrange("q (s u) -> q s u", u=2)
             for j0 in range(0, count, 2):
@@ -102,7 +104,7 @@ def tile_timesformerlayer_pc_t_kernel(
                 for j in range(n):
                     for u in range(2):
                         nc.tensor.transpose(
-                            flipped[:, j, u, :], words[:, j0 + j, u:WORDS:2], identity[:]
+                            flipped[:, j, u, :], split[:, j0 + j, u, :], identity[:]
                         )
                 nc.scalar.copy(
                     out=grouped_words[:, j0 * P : (j0 + n) * P, :].rearrange(

from contextlib import ExitStack

import concourse.mybir as mybir
from concourse.masks import make_identity

F32 = mybir.dt.float32
BF16 = mybir.dt.bfloat16
I32 = mybir.dt.int32
U32 = mybir.dt.uint32
U8 = mybir.dt.uint8
FP8X4 = mybir.dt.float8_e4m3fn_x4
FP4X4 = mybir.dt.float4_e2m1fn_x4
ADD = mybir.AluOpType.add
MULT = mybir.AluOpType.mult

P = 128
SAMPLES = 16
FRAMES = 8
PATCHES = 36
POSITIONS = 1 + PATCHES
WIDTH = 512
PACK = 4
WORDS = WIDTH // 2
BATCH = 4
BATCHES = [(0, 1)] + [(first, BATCH) for first in range(1, POSITIONS, BATCH)]
VECTOR_EVERY = 3

FLOPS = 2 * P * POSITIONS * WIDTH * WIDTH


def tile_timesformerlayer_pc_t_kernel(
    tc, ctx_s, x_res, s_out_w_words, s_out_w_scales, s_out_b, out
):
    nc = tc.nc
    with ExitStack() as stack:
        resident = stack.enter_context(tc.tile_pool(name="resident", bufs=1))
        staging = stack.enter_context(tc.tile_pool(name="staging", bufs=3))
        bias_bank = stack.enter_context(tc.psum_pool(name="bias_bank", bufs=1))
        flipped_banks = stack.enter_context(tc.psum_pool(name="flipped_banks", bufs=3))
        product_banks = stack.enter_context(tc.psum_pool(name="product_banks", bufs=4))

        ctx_tiles = [
            resident.tile([P, count, WIDTH], BF16, name="ctx%d" % first)
            for first, count in BATCHES
        ]
        xres_tiles = [resident.tile([P, WIDTH], BF16, name="xres%d" % p) for p in range(PATCHES)]
        sum_tiles = [resident.tile([P, WIDTH], F32, name="sum%d" % p) for p in range(PATCHES)]

        nc.sync.dma_start(out=ctx_tiles[0][:], in_=ctx_s[:, 0:1, :])

        w_words = resident.tile([P, 2 * WIDTH], U8, align_bytes=64)
        nc.sync.dma_start(out=w_words[:].bitcast(I32), in_=s_out_w_words[0].bitcast(I32))
        w_scales = resident.tile([P, WIDTH], U8, align_bytes=64)
        nc.vector.memset(w_scales[:].bitcast(I32), 0)
        for quadrant in range(4):
            nc.sync.dma_start(
                out=w_scales[32 * quadrant : 32 * quadrant + 4, :].bitcast(I32),
                in_=s_out_w_scales[0, 4 * quadrant : 4 * quadrant + 4, :].bitcast(I32),
            )

        bias_row = resident.tile([P, WIDTH], BF16)
        nc.vector.memset(bias_row[:], 0.0)
        nc.sync.dma_start(out=bias_row[0:1, :], in_=s_out_b.unsqueeze(0))
        xres_class = resident.tile([SAMPLES, WIDTH], BF16)
        nc.sync.dma_start(out=xres_class[:], in_=x_res[:, 0, :])

        for i in range(1, len(BATCHES)):
            first, count = BATCHES[i]
            nc.sync.dma_start(out=ctx_tiles[i][:], in_=ctx_s[:, first : first + count, :])
            for p in range(first - 1, first - 1 + count):
                nc.sync.dma_start(
                    out=xres_tiles[p][:], in_=x_res[:, 1 + FRAMES * p : 1 + FRAMES * (p + 1), :]
                )

        identity = resident.tile([P, P], F32)
        make_identity(nc, identity[:])

        ones = resident.tile([P, P], BF16)
        nc.vector.memset(ones[:], 1.0)
        bias_psum = bias_bank.tile([P, WIDTH], F32)
        nc.tensor.matmul(out=bias_psum[:], lhsT=ones[:], rhs=bias_row[:], start=True, stop=True)
        bias_sbuf = resident.tile([P, WIDTH], F32)
        nc.vector.tensor_copy(out=bias_sbuf[:], in_=bias_psum[:])

        same_sample = resident.tile([P, P], F32)
        nc.vector.memset(same_sample[:], 0.0)
        nc.vector.tensor_reduce(
            out=same_sample[:, 0:SAMPLES],
            in_=identity[:].rearrange("k (b t) -> k b t", t=FRAMES),
            axis=mybir.AxisListType.X,
            op=ADD,
        )

        def transpose_batch(i):
            count = BATCHES[i][1]
            words = ctx_tiles[i][:].bitcast(F32)
            split = staging.tile([P, count, 2, P], F32, tag="split")
            nc.scalar.copy(out=split[:], in_=words.rearrange("s j (q u) -> s j u q", u=2))
            grouped = staging.tile([P, count * P * PACK], BF16, tag="grouped", align_bytes=64)
            grouped_words = grouped[:].bitcast(F32).rearrange("q (s u) -> q s u", u=2)
            for j0 in range(0, count, 2):
                n = min(2, count - j0)
                flipped = flipped_banks.tile([P, 2, 2, P], F32, tag="flipped")
                for j in range(n):
                    for u in range(2):
                        nc.tensor.transpose(
                            flipped[:, j, u, :], split[:, j0 + j, u, :], identity[:]
                        )
                nc.scalar.copy(
                    out=grouped_words[:, j0 * P : (j0 + n) * P, :].rearrange(
                        "q (j s) u -> q j s u", j=n
                    ),
                    in_=flipped[:, 0:n].rearrange("q j u s -> q j s u"),
                )
            return grouped

        def quantise_batch(i, grouped):
            count = BATCHES[i][1]
            codes = staging.tile([P, count * P], U32, tag="codes", align_bytes=64)
            scales = staging.tile([P, count * P], U8, tag="scales", align_bytes=64)
            nc.vector.quantize_mx(out=codes[:].bitcast(FP8X4), scales=scales[:], in_=grouped[:])
            return codes, scales

        def multiply(quantised, j):
            codes, scales = quantised
            tokens = slice(j * P, (j + 1) * P)
            product = product_banks.tile([P, WIDTH], F32, tag="product")
            nc.tensor.matmul_mx(
                out=product[:],
                lhsT=codes[:, tokens].bitcast(FP8X4),
                lhsT_scale=scales[:, tokens],
                rhs=w_words[:].bitcast(FP4X4),
                rhs_scale=w_scales[:],
                start=True,
                stop=True,
            )
            return product

        def add_bias(p):
            if p % VECTOR_EVERY == 0:
                nc.vector.tensor_tensor(
                    out=sum_tiles[p][:], in0=bias_psum[:], in1=xres_tiles[p][:], op=ADD
                )
            else:
                nc.gpsimd.tensor_tensor(
                    out=sum_tiles[p][:], in0=xres_tiles[p][:], in1=bias_sbuf[:], op=ADD
                )

        def finish_patch(p, product):
            nc.vector.tensor_tensor(
                out=sum_tiles[p][:], in0=product[:], in1=sum_tiles[p][:], op=ADD
            )
            nc.sync.dma_start(
                out=out[:, 1 + FRAMES * p : 1 + FRAMES * (p + 1), :], in_=sum_tiles[p][:]
            )

        def finish_class_token(product):
            class_res = resident.tile([P, WIDTH], F32)
            nc.scalar.copy(out=class_res[:], in_=product[:])
            frame_sum = product_banks.tile([P, WIDTH], F32, tag="product")
            nc.tensor.matmul(
                out=frame_sum[:], lhsT=same_sample[:], rhs=class_res[:], start=True, stop=True
            )
            class_sum = resident.tile([SAMPLES, WIDTH], F32)
            nc.vector.tensor_tensor(
                out=class_sum[:], in0=bias_psum[0:SAMPLES, :], in1=xres_class[:], op=ADD
            )
            nc.vector.scalar_tensor_tensor(
                out=class_sum[:],
                in0=frame_sum[0:SAMPLES, :],
                scalar=1.0 / FRAMES,
                in1=class_sum[:],
                op0=MULT,
                op1=ADD,
            )
            nc.sync.dma_start(out=out[:, 0, :], in_=class_sum[:])

        last = len(BATCHES) - 1
        grouped_tiles = {0: transpose_batch(0), 1: transpose_batch(1)}
        products = [multiply(quantise_batch(0, grouped_tiles[0]), 0)]
        for i in range(len(BATCHES)):
            first, count = BATCHES[i]
            if i + 2 <= last:
                grouped_tiles[i + 2] = transpose_batch(i + 2)
            if i + 1 <= last:
                quantised = quantise_batch(i + 1, grouped_tiles[i + 1])
                for j in range(BATCH):
                    add_bias(BATCHES[i + 1][0] - 1 + j)
            if i == 0:
                finish_class_token(products[0])
            else:
                for j in range(count):
                    finish_patch(first - 1 + j, products[j])
            if i + 1 <= last:
                products = [multiply(quantised, j) for j in range(BATCH)]
